import numpy as np
import ml_dtypes


def mxq(x, axis, fmt="e4m3"):
    dtype, down = {"e4m3": (ml_dtypes.float8_e4m3fn, 7), "e5m2": (ml_dtypes.float8_e5m2, 14)}[fmt]
    v = np.moveaxis(np.asarray(x, np.float32).astype(ml_dtypes.bfloat16).astype(np.float64), axis, -1)
    blocks = v.reshape(v.shape[:-1] + (-1, 32))
    amax = np.abs(blocks).max(-1, keepdims=True)
    byte = np.maximum(np.where(amax > 0, np.frexp(amax)[1] - 1 + 127, 0) - down, 1)
    scale = np.exp2(byte - 127.0)
    codes = (blocks / scale).astype(np.float32).astype(dtype).astype(np.float64)
    return np.moveaxis((codes * scale).reshape(v.shape), -1, axis)


WIDE = False


def mx_kscale(k):
    if not WIDE:
        return np.ones(k)
    levels = np.array([10, -10, 5, -5, 0])
    if k % 512:
        return np.exp2(np.random.permutation(np.resize(levels, k // 32))).repeat(32)
    a = np.empty((k // 512, 16))
    for p in range(k // 512):
        a[p, :8] = np.random.permutation(np.resize(levels, 8))
        for g in range(8):
            far = levels[np.abs(levels - a[p, g]) >= 10]
            a[p, g + 8] = far[np.random.randint(len(far))]
    return np.exp2(a.ravel()).repeat(32)


BF16 = ml_dtypes.bfloat16


def bf(x):
    return np.asarray(x, np.float32).astype(BF16)


def f64(x):
    return np.asarray(x).astype(np.float64)


C, P, B, D = 3, 512, 2, 64
N = C * P
ID = C // 2


def laplacian_with_self_loop(adj):
    a = adj + np.eye(adj.shape[0])
    d_inv_sqrt = 1.0 / np.sqrt(a.sum(axis=1))
    return d_inv_sqrt[:, None] * a * d_inv_sqrt[None, :]


def setup_inputs():
    s = mx_kscale(P)
    sp = s / s.min()
    r = np.exp2(np.random.uniform(-1.0, 1.0, N))
    adj = np.random.uniform(0.0, 1.0, (N, N)) * r[:, None] * np.tile(sp, C)[None, :]
    x = np.random.standard_normal((P, B * D)) * (0.15 * N * sp.mean() / np.sqrt(P / 3.0)) / sp[:, None]
    return {"globalAdj": bf(adj), "inputs": bf(x), "batch_size": B, "output_dim": D, "id": ID}


def reference(globalAdj, inputs, batch_size, output_dim, id):
    lap = laplacian_with_self_loop(f64(globalAdj))
    col = lap[:, id * P:(id + 1) * P]
    out = mxq(col, 1, "e4m3") @ mxq(f64(inputs), 0, "e4m3")
    out = out.reshape(N, batch_size, output_dim)
    return out.transpose(1, 0, 2)

@@ -1,0 +1,138 @@
+import concourse.mybir as mybir
+from concourse.masks import make_identity
+
+BF16 = mybir.dt.bfloat16
+F32 = mybir.dt.float32
+U32 = mybir.dt.uint32
+U8 = mybir.dt.uint8
+FP8X4 = mybir.dt.float8_e4m3fn_x4
+ALU = mybir.AluOpType
+ACT = mybir.ActivationFunctionType
+
+P = 128
+PACK = 4
+NODES = 1536
+CLIENT = P * PACK
+FEATURES = 128
+ROW_TILES = NODES // P
+HALF = NODES // 2
+
+FLOPS = 2 * NODES * CLIENT * FEATURES
+
+
+def tile_gcn_s_kernel(tc, globalAdj, inputs, batch_size, output_dim, client, out):
+    nc = tc.nc
+    assert batch_size * output_dim == FEATURES
+
+    own = list(range(PACK * client, PACK * client + PACK))
+    order = own + [r for r in range(ROW_TILES) if r not in own]
+    mine = slice(client * CLIENT, (client + 1) * CLIENT)
+    own_rows = globalAdj[mine, :].rearrange("(p t) j -> p t j", t=PACK)
+    own_out = out[:, mine, :].rearrange("b (n t) f -> n t b f", t=PACK)
+
+    with tc.tile_pool(name="keep", bufs=1) as keep, tc.tile_pool(name="sums", bufs=ROW_TILES) as sums, tc.tile_pool(
+        name="work", bufs=4
+    ) as work, tc.psum_pool(name="turned", bufs=5) as turned_pool, tc.psum_pool(name="product", bufs=3) as product_pool:
+        x_raw = keep.tile([P, PACK, FEATURES], BF16)
+        nc.scalar.dma_start(out=x_raw[:], in_=inputs.rearrange("(p t) f -> p t f", t=PACK))
+        adj = []
+        for i in range(ROW_TILES):
+            rows = keep.tile([P, NODES], BF16, name="adj%d" % i)
+            if i < PACK:
+                nc.sync.dma_start(out=rows[:], in_=own_rows[:, i, :])
+            else:
+                nc.sync.dma_start(out=rows[:], in_=globalAdj[order[i] * P : (order[i] + 1) * P, :])
+            adj.append(rows)
+
+        ident = keep.tile([P, P], F32)
+        make_identity(nc, ident[:])
+        one = keep.tile([P, 1], F32)
+        nc.vector.memset(one[:], 1.0)
+        warm = keep.tile([P, 1], F32)
+        nc.scalar.activation(out=warm[:], in_=one[:], func=ACT.Sqrt)
+
+        x_grouped = keep.tile([P, FEATURES, PACK], BF16, align_bytes=64)
+        nc.vector.tensor_copy(out=x_grouped[:], in_=x_raw[:].rearrange("p t f -> p f t"))
+        x_codes = keep.tile([P, FEATURES], U32, align_bytes=64)
+        x_scales = keep.tile([P, FEATURES], U8, align_bytes=64)
+        nc.vector.quantize_mx(
+            out=x_codes[:].bitcast(FP8X4), scales=x_scales[:], in_=x_grouped[:].rearrange("p f t -> p (f t)")
+        )
+
+        degree = keep.tile([P, ROW_TILES, 8], F32)
+        root = keep.tile([P, ROW_TILES], F32)
+        dinv = keep.tile([P, ROW_TILES], F32)
+
+        turned = {}
+
+        def front(i):
+            if i % 3 == 2:
+                unused = sums.tile([P, NODES], BF16, name="unused_s")
+                nc.scalar.activation(out=unused[:], in_=adj[i][:], func=ACT.Copy, accum_out=degree[:, i, 0:1])
+            else:
+                unused = sums.tile([P, HALF], F32, name="unused_v")
+                nc.vector.scalar_tensor_tensor(
+                    out=unused[:],
+                    in0=adj[i][:, 0:HALF],
+                    scalar=1.0,
+                    in1=adj[i][:, HALF:NODES],
+                    op0=ALU.mult,
+                    op1=ALU.add,
+                    accum_out=degree[:, i, 0:1],
+                )
+            nc.scalar.activation(out=root[:, i : i + 1], in_=degree[:, i, 0:1], func=ACT.Sqrt, bias=1.0)
+            nc.vector.reciprocal(out=dinv[:, i : i + 1], in_=root[:, i : i + 1])
+            scaled = work.tile([P, CLIENT], F32)
+            nc.scalar.activation(
+                out=scaled[:].rearrange("n (t p) -> n t p", t=PACK),
+                in_=adj[i][:, mine].rearrange("n (p t) -> n t p", t=PACK),
+                func=ACT.Copy,
+                scale=dinv[:, i : i + 1],
+            )
+            if i < PACK:
+                block = scaled[:, i * P : (i + 1) * P]
+                nc.vector.scalar_tensor_tensor(
+                    out=block, in0=ident[:], scalar=dinv[:, i : i + 1], in1=block, op0=ALU.mult, op1=ALU.add
+                )
+            bank = turned_pool.tile([P, PACK, P], F32)
+            for t in range(PACK):
+                nc.tensor.transpose(bank[:, t, :], scaled[:, t * P : (t + 1) * P], ident[:])
+            turned[i] = bank
+
+        def back(i):
+            grouped = work.tile([P, P, PACK], BF16, align_bytes=64)
+            nc.vector.tensor_tensor(
+                out=grouped[:],
+                in0=turned[i][:].rearrange("p t n -> p n t"),
+                in1=dinv[:, 0:PACK].unsqueeze(1).to_broadcast([P, P, PACK]),
+                op=ALU.mult,
+            )
+            codes = work.tile([P, P], U32, align_bytes=64)
+            scales = work.tile([P, P], U8, align_bytes=64)
+            nc.vector.quantize_mx(
+                out=codes[:].bitcast(FP8X4), scales=scales[:], in_=grouped[:].rearrange("p n t -> p (n t)")
+            )
+            product = product_pool.tile([P, FEATURES], F32)
+            nc.tensor.matmul_mx(
+                out=product[:],
+                lhsT=codes[:].bitcast(FP8X4),
+                lhsT_scale=scales[:],
+                rhs=x_codes[:].bitcast(FP8X4),
+                rhs_scale=x_scales[:],
+                start=True,
+                stop=True,
+            )
+            y = work.tile([P, FEATURES], F32)
+            nc.scalar.copy(out=y[:], in_=product[:])
+            r = order[i]
+            rows_out = own_out[:, i, :, :] if i < PACK else out[:, r * P : (r + 1) * P, :].rearrange("b n f -> n b f")
+            nc.sync.dma_start(
+                out=rows_out,
+                in_=y[:].rearrange("n (b f) -> n b f", b=batch_size),
+            )
+
+        for i in range(ROW_TILES + PACK):
+            if i < ROW_TILES:
+                front(i)
+            if i >= PACK:
+                back(i - PACK)

@@ -15,7 +15,7 @@ NODES = 1536
 CLIENT = P * PACK
 FEATURES = 128
 ROW_TILES = NODES // P
-HALF = NODES // 2
+SHARE = 1024
 
 FLOPS = 2 * NODES * CLIENT * FEATURES
 
@@ -24,115 +24,172 @@ def tile_gcn_s_kernel(tc, globalAdj, inputs, batch_size, output_dim, client, out
     nc = tc.nc
     assert batch_size * output_dim == FEATURES
 
-    own = list(range(PACK * client, PACK * client + PACK))
-    order = own + [r for r in range(ROW_TILES) if r not in own]
+    clients = [client] + [c for c in range(NODES // CLIENT) if c != client]
     mine = slice(client * CLIENT, (client + 1) * CLIENT)
-    own_rows = globalAdj[mine, :].rearrange("(p t) j -> p t j", t=PACK)
-    own_out = out[:, mine, :].rearrange("b (n t) f -> n t b f", t=PACK)
 
-    with tc.tile_pool(name="keep", bufs=1) as keep, tc.tile_pool(name="sums", bufs=ROW_TILES) as sums, tc.tile_pool(
+    def client_rows(i):
+        c = clients[i // PACK]
+        return slice(c * CLIENT, (c + 1) * CLIENT)
+
+    split = (0, 1, 2, 3, ROW_TILES - 1)
+    on_vector = (5, 8)
+
+    with tc.tile_pool(name="keep", bufs=1) as keep, tc.tile_pool(name="sums", bufs=2) as sums, tc.tile_pool(
         name="work", bufs=4
-    ) as work, tc.psum_pool(name="turned", bufs=5) as turned_pool, tc.psum_pool(name="product", bufs=3) as product_pool:
-        x_raw = keep.tile([P, PACK, FEATURES], BF16)
-        nc.scalar.dma_start(out=x_raw[:], in_=inputs.rearrange("(p t) f -> p t f", t=PACK))
-        adj = []
-        for i in range(ROW_TILES):
-            rows = keep.tile([P, NODES], BF16, name="adj%d" % i)
-            if i < PACK:
-                nc.sync.dma_start(out=rows[:], in_=own_rows[:, i, :])
-            else:
-                nc.sync.dma_start(out=rows[:], in_=globalAdj[order[i] * P : (order[i] + 1) * P, :])
-            adj.append(rows)
+    ) as work, tc.psum_pool(name="turned", bufs=4) as turned_pool, tc.psum_pool(name="product", bufs=1) as product_pool:
+        adj = [keep.tile([P, NODES], BF16, name="adj%d" % i) for i in range(ROW_TILES)]
+        x_raw = keep.tile([P, PACK, FEATURES], BF16, name="x_raw")
+        ident = keep.tile([P, P], F32, name="ident")
+        one = keep.tile([P, 1], F32, name="one")
+        warm = keep.tile([P, 1], F32, name="warm")
+        x_grouped = keep.tile([P, FEATURES, PACK], BF16, align_bytes=64, name="x_grouped")
+        x_codes = keep.tile([P, FEATURES], U32, align_bytes=64, name="x_codes")
+        x_scales = keep.tile([P, FEATURES], U8, align_bytes=64, name="x_scales")
+        sum_v = keep.tile([P, ROW_TILES, 8], F32, name="sum_v")
+        sum_s = keep.tile([P, ROW_TILES, 8], F32, name="sum_s")
+        dinv = keep.tile([P, ROW_TILES], F32, name="dinv")
 
-        ident = keep.tile([P, P], F32)
-        make_identity(nc, ident[:])
-        one = keep.tile([P, 1], F32)
-        nc.vector.memset(one[:], 1.0)
-        warm = keep.tile([P, 1], F32)
-        nc.scalar.activation(out=warm[:], in_=one[:], func=ACT.Sqrt)
+        runs = [range(0, 4), range(4, 8), range(8, 11), range(11, 12)]
+        banks = [product_pool.tile([P, len(run), FEATURES], F32, name="product%d" % g) for g, run in enumerate(runs)]
 
-        x_grouped = keep.tile([P, FEATURES, PACK], BF16, align_bytes=64)
-        nc.vector.tensor_copy(out=x_grouped[:], in_=x_raw[:].rearrange("p t f -> p f t"))
-        x_codes = keep.tile([P, FEATURES], U32, align_bytes=64)
-        x_scales = keep.tile([P, FEATURES], U8, align_bytes=64)
-        nc.vector.quantize_mx(
-            out=x_codes[:].bitcast(FP8X4), scales=x_scales[:], in_=x_grouped[:].rearrange("p f t -> p (f t)")
-        )
+        scaled, turned, grouped, codes, scales = {}, {}, {}, {}, {}
 
-        degree = keep.tile([P, ROW_TILES, 8], F32)
-        root = keep.tile([P, ROW_TILES], F32)
-        dinv = keep.tile([P, ROW_TILES], F32)
+        def load(i):
+            rows = globalAdj[client_rows(i), :].rearrange("(p t) j -> p t j", t=PACK)
+            nc.sync.dma_start(out=adj[i][:], in_=rows[:, i % PACK, :])
 
-        turned = {}
-
-        def front(i):
-            if i % 3 == 2:
-                unused = sums.tile([P, NODES], BF16, name="unused_s")
-                nc.scalar.activation(out=unused[:], in_=adj[i][:], func=ACT.Copy, accum_out=degree[:, i, 0:1])
-            else:
-                unused = sums.tile([P, HALF], F32, name="unused_v")
-                nc.vector.scalar_tensor_tensor(
-                    out=unused[:],
-                    in0=adj[i][:, 0:HALF],
-                    scalar=1.0,
-                    in1=adj[i][:, HALF:NODES],
-                    op0=ALU.mult,
-                    op1=ALU.add,
-                    accum_out=degree[:, i, 0:1],
-                )
-            nc.scalar.activation(out=root[:, i : i + 1], in_=degree[:, i, 0:1], func=ACT.Sqrt, bias=1.0)
-            nc.vector.reciprocal(out=dinv[:, i : i + 1], in_=root[:, i : i + 1])
-            scaled = work.tile([P, CLIENT], F32)
-            nc.scalar.activation(
-                out=scaled[:].rearrange("n (t p) -> n t p", t=PACK),
-                in_=adj[i][:, mine].rearrange("n (p t) -> n t p", t=PACK),
-                func=ACT.Copy,
-                scale=dinv[:, i : i + 1],
+        def sum_on_vector(i, columns):
+            unused = sums.tile([P, NODES], BF16, name="unused_v")
+            nc.vector.tensor_scalar(
+                out=unused[:, columns],
+                in0=adj[i][:, columns],
+                scalar1=1.0,
+                scalar2=1.0,
+                op0=ALU.mult,
+                op1=ALU.add,
+                accum_out=sum_v[:, i, 0:1],
             )
-            if i < PACK:
-                block = scaled[:, i * P : (i + 1) * P]
-                nc.vector.scalar_tensor_tensor(
-                    out=block, in0=ident[:], scalar=dinv[:, i : i + 1], in1=block, op0=ALU.mult, op1=ALU.add
-                )
-            bank = turned_pool.tile([P, PACK, P], F32)
-            for t in range(PACK):
-                nc.tensor.transpose(bank[:, t, :], scaled[:, t * P : (t + 1) * P], ident[:])
-            turned[i] = bank
 
-        def back(i):
-            grouped = work.tile([P, P, PACK], BF16, align_bytes=64)
+        def sum_on_scalar(i, columns):
+            unused = sums.tile([P, NODES], BF16, name="unused_s")
+            nc.scalar.activation(out=unused[:, columns], in_=adj[i][:, columns], func=ACT.Copy, accum_out=sum_s[:, i, 0:1])
+
+        def row_sum(i):
+            if i in split:
+                sum_on_vector(i, slice(0, SHARE))
+                sum_on_scalar(i, slice(SHARE, NODES))
+            elif i in on_vector:
+                sum_on_vector(i, slice(0, NODES))
+            else:
+                sum_on_scalar(i, slice(0, NODES))
+
+        def inverse_root(i):
+            source, bias = sum_v, 0.0
+            if i in split:
+                bias = sum_s[:, i, 0:1]
+            elif i not in on_vector:
+                source, bias = sum_s, 1.0
+            nc.scalar.activation(out=dinv[:, i : i + 1], in_=source[:, i, 0:1], func=ACT.Abs_reciprocal_sqrt, bias=bias)
+
+        def scale_rows(i, engine):
+            scaled[i] = work.tile([P, PACK, P], F32, name="scaled")
+            engine.tensor_scalar(
+                out=scaled[i][:],
+                in0=adj[i][:, mine].rearrange("n (p t) -> n t p", t=PACK),
+                scalar1=dinv[:, i : i + 1],
+                scalar2=0.0,
+                op0=ALU.mult,
+                op1=ALU.add,
+            )
+
+        def self_loop(i):
+            block = scaled[i][:, i, :]
+            nc.vector.scalar_tensor_tensor(
+                out=block, in0=ident[:], scalar=dinv[:, i : i + 1], in1=block, op0=ALU.mult, op1=ALU.add
+            )
+
+        def turn(i):
+            turned[i] = turned_pool.tile([P, PACK, P], F32, name="turned")
+            for t in range(PACK):
+                nc.tensor.transpose(turned[i][:, t, :], scaled[i][:, t, :], ident[:])
+
+        def scale_columns(i):
+            grouped[i] = work.tile([P, P, PACK], BF16, align_bytes=64, name="grouped")
             nc.vector.tensor_tensor(
-                out=grouped[:],
+                out=grouped[i][:],
                 in0=turned[i][:].rearrange("p t n -> p n t"),
                 in1=dinv[:, 0:PACK].unsqueeze(1).to_broadcast([P, P, PACK]),
                 op=ALU.mult,
             )
-            codes = work.tile([P, P], U32, align_bytes=64)
-            scales = work.tile([P, P], U8, align_bytes=64)
+
+        def quantise(i):
+            codes[i] = work.tile([P, P], U32, align_bytes=64, name="codes")
+            scales[i] = work.tile([P, P], U8, align_bytes=64, name="scales")
             nc.vector.quantize_mx(
-                out=codes[:].bitcast(FP8X4), scales=scales[:], in_=grouped[:].rearrange("p n t -> p (n t)")
+                out=codes[i][:].bitcast(FP8X4), scales=scales[i][:], in_=grouped[i][:].rearrange("p n t -> p (n t)")
             )
-            product = product_pool.tile([P, FEATURES], F32)
+
+        def multiply(i):
+            g = [i in run for run in runs].index(True)
             nc.tensor.matmul_mx(
-                out=product[:],
-                lhsT=codes[:].bitcast(FP8X4),
-                lhsT_scale=scales[:],
+                out=banks[g][:, i - runs[g][0], :],
+                lhsT=codes[i][:].bitcast(FP8X4),
+                lhsT_scale=scales[i][:],
                 rhs=x_codes[:].bitcast(FP8X4),
                 rhs_scale=x_scales[:],
                 start=True,
                 stop=True,
             )
-            y = work.tile([P, FEATURES], F32)
-            nc.scalar.copy(out=y[:], in_=product[:])
-            r = order[i]
-            rows_out = own_out[:, i, :, :] if i < PACK else out[:, r * P : (r + 1) * P, :].rearrange("b n f -> n b f")
-            nc.sync.dma_start(
-                out=rows_out,
-                in_=y[:].rearrange("n (b f) -> n b f", b=batch_size),
-            )
 
-        for i in range(ROW_TILES + PACK):
-            if i < ROW_TILES:
-                front(i)
-            if i >= PACK:
-                back(i - PACK)
+        def store(g):
+            n, first = len(runs[g]), runs[g][0]
+            y = keep.tile([P, batch_size, n, output_dim], F32, name="y%d" % g)
+            nc.scalar.copy(out=y[:].rearrange("p b t f -> p t b f"), in_=banks[g][:].rearrange("p t (b f) -> p t b f", b=batch_size))
+            rows = out[:, client_rows(first), :].rearrange("b (p t) f -> p b t f", t=PACK)
+            nc.sync.dma_start(out=rows[:, :, first % PACK : first % PACK + n, :], in_=y[:])
+
+        make_identity(nc, ident[:])
+        with tc.manual_schedule():
+            nc.sync.dma_start(out=x_raw[:], in_=inputs.rearrange("(p t) f -> p t f", t=PACK))
+            for i in range(ROW_TILES):
+                load(i)
+            nc.vector.memset(one[:], 1.0)
+            nc.scalar.activation(out=warm[:], in_=one[:], func=ACT.Abs_reciprocal_sqrt)
+
+            nc.vector.tensor_copy(out=x_grouped[:], in_=x_raw[:].rearrange("p t f -> p f t"))
+            nc.vector.quantize_mx(
+                out=x_codes[:].bitcast(FP8X4), scales=x_scales[:], in_=x_grouped[:].rearrange("p f t -> p (f t)")
+            )
+            for i in range(PACK):
+                row_sum(i)
+                inverse_root(i)
+                scale_rows(i, nc.gpsimd)
+                if i >= 2:
+                    self_loop(i - 2)
+                    turn(i - 2)
+            scale_columns(0)
+            self_loop(2)
+            for i in range(ROW_TILES + 1):
+                if i + 4 < ROW_TILES:
+                    row_sum(i + 4)
+                if i + 4 < ROW_TILES and i + 4 not in on_vector:
+                    if i + 3 in on_vector:
+                        inverse_root(i + 3)
+                    inverse_root(i + 4)
+                    if i + 3 in on_vector:
+                        scale_rows(i + 3, nc.gpsimd)
+                    scale_rows(i + 4, nc.gpsimd)
+                if i == 0:
+                    turn(2)
+                if i == 1:
+                    self_loop(3)
+                    turn(3)
+                if 4 <= i + 3 < ROW_TILES:
+                    turn(i + 3)
+                if 1 <= i < ROW_TILES:
+                    scale_columns(i)
+                if i >= 1:
+                    quantise(i - 1)
+                    multiply(i - 1)
+            for g in range(len(runs)):
+                store(g)

@@ -52,7 +52,7 @@ def tile_gcn_s_kernel(tc, globalAdj, inputs, batch_size, output_dim, client, out
         runs = [range(0, 4), range(4, 8), range(8, 11), range(11, 12)]
         banks = [product_pool.tile([P, len(run), FEATURES], F32, name="product%d" % g) for g, run in enumerate(runs)]
 
-        scaled, turned, grouped, codes, scales = {}, {}, {}, {}, {}
+        scaled, turned, whole, grouped, codes, scales = {}, {}, {}, {}, {}, {}
 
         def load(i):
             rows = globalAdj[client_rows(i), :].rearrange("(p t) j -> p t j", t=PACK)
@@ -114,27 +114,39 @@ def tile_gcn_s_kernel(tc, globalAdj, inputs, batch_size, output_dim, client, out
                 nc.tensor.transpose(turned[i][:, t, :], scaled[i][:, t, :], ident[:])
 
         def scale_columns(i):
-            grouped[i] = work.tile([P, P, PACK], BF16, align_bytes=64, name="grouped")
+            if i % 2 == 0:
+                pair = work.tile([P, 2, P, PACK], BF16, align_bytes=64, name="pair")
+                pair_codes = work.tile([P, 2, P], U32, align_bytes=64, name="pair_codes")
+                pair_scales = work.tile([P, 2, P], U8, align_bytes=64, name="pair_scales")
+                for j in range(2):
+                    grouped[i + j], codes[i + j], scales[i + j] = pair[:, j], pair_codes[:, j, :], pair_scales[:, j, :]
+                whole[i] = (pair, pair_codes, pair_scales)
             nc.vector.tensor_tensor(
-                out=grouped[i][:],
+                out=grouped[i],
                 in0=turned[i][:].rearrange("p t n -> p n t"),
                 in1=dinv[:, 0:PACK].unsqueeze(1).to_broadcast([P, P, PACK]),
                 op=ALU.mult,
             )
 
-        def quantise(i):
-            codes[i] = work.tile([P, P], U32, align_bytes=64, name="codes")
-            scales[i] = work.tile([P, P], U8, align_bytes=64, name="scales")
+        def quantise_pair(i):
+            pair, pair_codes, pair_scales = whole[i]
             nc.vector.quantize_mx(
-                out=codes[i][:].bitcast(FP8X4), scales=scales[i][:], in_=grouped[i][:].rearrange("p n t -> p (n t)")
+                out=pair_codes[:].rearrange("p j n -> p (j n)").bitcast(FP8X4),
+                scales=pair_scales[:].rearrange("p j n -> p (j n)"),
+                in_=pair[:].rearrange("p j n t -> p (j n t)"),
+            )
+
+        def quantise(i):
+            nc.vector.quantize_mx(
+                out=codes[i].bitcast(FP8X4), scales=scales[i], in_=grouped[i].rearrange("p n t -> p (n t)")
             )
 
         def multiply(i):
             g = [i in run for run in runs].index(True)
             nc.tensor.matmul_mx(
                 out=banks[g][:, i - runs[g][0], :],
-                lhsT=codes[i][:].bitcast(FP8X4),
-                lhsT_scale=scales[i][:],
+                lhsT=codes[i].bitcast(FP8X4),
+                lhsT_scale=scales[i],
                 rhs=x_codes[:].bitcast(FP8X4),
                 rhs_scale=x_scales[:],
                 start=True,
@@ -188,8 +200,13 @@ def tile_gcn_s_kernel(tc, globalAdj, inputs, batch_size, output_dim, client, out
                     turn(i + 3)
                 if 1 <= i < ROW_TILES:
                     scale_columns(i)
-                if i >= 1:
-                    quantise(i - 1)
+                if i in (2, 4, 6, 8, 10):
+                    quantise_pair(i - 2)
+                    multiply(i - 2)
                     multiply(i - 1)
+                if i == ROW_TILES:
+                    for j in (i - 2, i - 1):
+                        quantise(j)
+                        multiply(j)
             for g in range(len(runs)):
                 store(g)

@@ -15,7 +15,6 @@ NODES = 1536
 CLIENT = P * PACK
 FEATURES = 128
 ROW_TILES = NODES // P
-SHARE = 1024
 
 FLOPS = 2 * NODES * CLIENT * FEATURES
 
@@ -31,12 +30,11 @@ def tile_gcn_s_kernel(tc, globalAdj, inputs, batch_size, output_dim, client, out
         c = clients[i // PACK]
         return slice(c * CLIENT, (c + 1) * CLIENT)
 
-    split = (0, 1, 2, 3, ROW_TILES - 1)
-    on_vector = (5, 8)
+    share = {0: 1024, 1: 1024, 2: 1024, 3: 1024, 4: 0, 5: 1536, 6: 0, 7: 0, 8: 1536, 9: 0, 10: 768, 11: 1024}
 
     with tc.tile_pool(name="keep", bufs=1) as keep, tc.tile_pool(name="sums", bufs=2) as sums, tc.tile_pool(
         name="work", bufs=4
-    ) as work, tc.psum_pool(name="turned", bufs=4) as turned_pool, tc.psum_pool(name="product", bufs=1) as product_pool:
+    ) as work, tc.psum_pool(name="turned", bufs=5) as turned_pool, tc.psum_pool(name="product", bufs=1) as product_pool:
         adj = [keep.tile([P, NODES], BF16, name="adj%d" % i) for i in range(ROW_TILES)]
         x_raw = keep.tile([P, PACK, FEATURES], BF16, name="x_raw")
         ident = keep.tile([P, P], F32, name="ident")
@@ -49,9 +47,10 @@ def tile_gcn_s_kernel(tc, globalAdj, inputs, batch_size, output_dim, client, out
         sum_s = keep.tile([P, ROW_TILES, 8], F32, name="sum_s")
         dinv = keep.tile([P, ROW_TILES], F32, name="dinv")
 
-        runs = [range(0, 4), range(4, 8), range(8, 11), range(11, 12)]
-        banks = [product_pool.tile([P, len(run), FEATURES], F32, name="product%d" % g) for g, run in enumerate(runs)]
+        runs = [range(0, 4), range(4, 8), range(8, 10), range(10, 12)]
+        banks = [product_pool.tile([P, PACK, FEATURES], F32, name="product%d" % c) for c in range(len(clients))]
 
+        looped = {}
         scaled, turned, whole, grouped, codes, scales = {}, {}, {}, {}, {}, {}
 
         def load(i):
@@ -75,19 +74,16 @@ def tile_gcn_s_kernel(tc, globalAdj, inputs, batch_size, output_dim, client, out
             nc.scalar.activation(out=unused[:, columns], in_=adj[i][:, columns], func=ACT.Copy, accum_out=sum_s[:, i, 0:1])
 
         def row_sum(i):
-            if i in split:
-                sum_on_vector(i, slice(0, SHARE))
-                sum_on_scalar(i, slice(SHARE, NODES))
-            elif i in on_vector:
-                sum_on_vector(i, slice(0, NODES))
-            else:
-                sum_on_scalar(i, slice(0, NODES))
+            if share[i] > 0:
+                sum_on_vector(i, slice(0, share[i]))
+            if share[i] < NODES:
+                sum_on_scalar(i, slice(share[i], NODES))
 
         def inverse_root(i):
             source, bias = sum_v, 0.0
-            if i in split:
+            if 0 < share[i] < NODES:
                 bias = sum_s[:, i, 0:1]
-            elif i not in on_vector:
+            elif share[i] == 0:
                 source, bias = sum_s, 1.0
             nc.scalar.activation(out=dinv[:, i : i + 1], in_=source[:, i, 0:1], func=ACT.Abs_reciprocal_sqrt, bias=bias)
 
@@ -106,6 +102,21 @@ def tile_gcn_s_kernel(tc, globalAdj, inputs, batch_size, output_dim, client, out
             block = scaled[i][:, i, :]
             nc.vector.scalar_tensor_tensor(
                 out=block, in0=ident[:], scalar=dinv[:, i : i + 1], in1=block, op0=ALU.mult, op1=ALU.add
+            )
+
+        def add_loop_early(i):
+            looped[i] = keep.tile([P, P], F32, name="looped%d" % i)
+            block = adj[i][:, mine].rearrange("n (p t) -> n t p", t=PACK)[:, i, :]
+            nc.gpsimd.tensor_tensor(out=looped[i][:], in0=block, in1=ident[:], op=ALU.add)
+
+        def scale_looped(i):
+            nc.gpsimd.tensor_scalar(
+                out=scaled[i][:, i, :],
+                in0=looped[i][:],
+                scalar1=dinv[:, i : i + 1],
+                scalar2=0.0,
+                op0=ALU.mult,
+                op1=ALU.add,
             )
 
         def turn(i):
@@ -142,9 +153,8 @@ def tile_gcn_s_kernel(tc, globalAdj, inputs, batch_size, output_dim, client, out
             )
 
         def multiply(i):
-            g = [i in run for run in runs].index(True)
             nc.tensor.matmul_mx(
-                out=banks[g][:, i - runs[g][0], :],
+                out=banks[i // PACK][:, i % PACK, :],
                 lhsT=codes[i].bitcast(FP8X4),
                 lhsT_scale=scales[i],
                 rhs=x_codes[:].bitcast(FP8X4),
@@ -156,57 +166,115 @@ def tile_gcn_s_kernel(tc, globalAdj, inputs, batch_size, output_dim, client, out
         def store(g):
             n, first = len(runs[g]), runs[g][0]
             y = keep.tile([P, batch_size, n, output_dim], F32, name="y%d" % g)
-            nc.scalar.copy(out=y[:].rearrange("p b t f -> p t b f"), in_=banks[g][:].rearrange("p t (b f) -> p t b f", b=batch_size))
+            nc.scalar.copy(out=y[:].rearrange("p b t f -> p t b f"), in_=banks[first // PACK][:, first % PACK : first % PACK + n, :].rearrange("p t (b f) -> p t b f", b=batch_size))
             rows = out[:, client_rows(first), :].rearrange("b (p t) f -> p b t f", t=PACK)
-            nc.sync.dma_start(out=rows[:, :, first % PACK : first % PACK + n, :], in_=y[:])
+            nc.scalar.dma_start(out=rows[:, :, first % PACK : first % PACK + n, :], in_=y[:])
 
         make_identity(nc, ident[:])
         with tc.manual_schedule():
+            load(0)
+            load(1)
+            load(2)
+            load(3)
             nc.sync.dma_start(out=x_raw[:], in_=inputs.rearrange("(p t) f -> p t f", t=PACK))
-            for i in range(ROW_TILES):
-                load(i)
+            load(4)
+            load(5)
+            load(6)
+            load(7)
+            load(8)
+            load(9)
+            load(10)
+            load(11)
             nc.vector.memset(one[:], 1.0)
             nc.scalar.activation(out=warm[:], in_=one[:], func=ACT.Abs_reciprocal_sqrt)
-
-            nc.vector.tensor_copy(out=x_grouped[:], in_=x_raw[:].rearrange("p t f -> p f t"))
-            nc.vector.quantize_mx(
-                out=x_codes[:].bitcast(FP8X4), scales=x_scales[:], in_=x_grouped[:].rearrange("p f t -> p (f t)")
-            )
-            for i in range(PACK):
-                row_sum(i)
-                inverse_root(i)
-                scale_rows(i, nc.gpsimd)
-                if i >= 2:
-                    self_loop(i - 2)
-                    turn(i - 2)
+            add_loop_early(0)
+            add_loop_early(1)
+            row_sum(0)
+            inverse_root(0)
+            scale_rows(0, nc.gpsimd)
+            scale_looped(0)
+            row_sum(1)
+            inverse_root(1)
+            scale_rows(1, nc.gpsimd)
+            scale_looped(1)
+            row_sum(2)
+            inverse_root(2)
+            scale_rows(2, nc.gpsimd)
+            turn(0)
+            row_sum(3)
+            inverse_root(3)
+            scale_rows(3, nc.gpsimd)
+            turn(1)
+            nc.gpsimd.tensor_scalar(out=x_grouped[:], in0=x_raw[:].rearrange("p t f -> p f t"), scalar1=1.0, scalar2=0.0, op0=ALU.mult, op1=ALU.add)
             scale_columns(0)
             self_loop(2)
-            for i in range(ROW_TILES + 1):
-                if i + 4 < ROW_TILES:
-                    row_sum(i + 4)
-                if i + 4 < ROW_TILES and i + 4 not in on_vector:
-                    if i + 3 in on_vector:
-                        inverse_root(i + 3)
-                    inverse_root(i + 4)
-                    if i + 3 in on_vector:
-                        scale_rows(i + 3, nc.gpsimd)
-                    scale_rows(i + 4, nc.gpsimd)
-                if i == 0:
-                    turn(2)
-                if i == 1:
-                    self_loop(3)
-                    turn(3)
-                if 4 <= i + 3 < ROW_TILES:
-                    turn(i + 3)
-                if 1 <= i < ROW_TILES:
-                    scale_columns(i)
-                if i in (2, 4, 6, 8, 10):
-                    quantise_pair(i - 2)
-                    multiply(i - 2)
-                    multiply(i - 1)
-                if i == ROW_TILES:
-                    for j in (i - 2, i - 1):
-                        quantise(j)
-                        multiply(j)
-            for g in range(len(runs)):
-                store(g)
+            row_sum(4)
+            inverse_root(4)
+            scale_rows(4, nc.gpsimd)
+            turn(2)
+            row_sum(5)
+            self_loop(3)
+            turn(3)
+            turn(4)
+            scale_columns(1)
+            nc.vector.quantize_mx(out=x_codes[:].bitcast(FP8X4), scales=x_scales[:], in_=x_grouped[:].rearrange("p f t -> p (f t)"))
+            inverse_root(5)
+            scale_rows(5, nc.gpsimd)
+            row_sum(6)
+            inverse_root(6)
+            scale_rows(6, nc.gpsimd)
+            turn(5)
+            scale_columns(2)
+            quantise_pair(0)
+            multiply(0)
+            multiply(1)
+            row_sum(7)
+            inverse_root(7)
+            scale_rows(7, nc.gpsimd)
+            turn(6)
+            scale_columns(3)
+            row_sum(8)
+            turn(7)
+            scale_columns(4)
+            quantise_pair(2)
+            multiply(2)
+            multiply(3)
+            inverse_root(8)
+            scale_rows(8, nc.gpsimd)
+            row_sum(9)
+            inverse_root(9)
+            scale_rows(9, nc.gpsimd)
+            turn(8)
+            scale_columns(5)
+            row_sum(10)
+            inverse_root(10)
+            scale_rows(10, nc.gpsimd)
+            turn(9)
+            scale_columns(6)
+            quantise_pair(4)
+            multiply(4)
+            multiply(5)
+            row_sum(11)
+            inverse_root(11)
+            scale_rows(11, nc.gpsimd)
+            turn(10)
+            scale_columns(7)
+            turn(11)
+            scale_columns(8)
+            quantise_pair(6)
+            multiply(6)
+            multiply(7)
+            scale_columns(9)
+            scale_columns(10)
+            quantise_pair(8)
+            multiply(8)
+            multiply(9)
+            scale_columns(11)
+            quantise(10)
+            multiply(10)
+            quantise(11)
+            multiply(11)
+            store(0)
+            store(1)
+            store(2)
+            store(3)

@@ -33,7 +33,7 @@ def tile_gcn_s_kernel(tc, globalAdj, inputs, batch_size, output_dim, client, out
     share = {0: 1024, 1: 1024, 2: 1024, 3: 1024, 4: 0, 5: 1536, 6: 0, 7: 0, 8: 1536, 9: 0, 10: 768, 11: 1024}
 
     with tc.tile_pool(name="keep", bufs=1) as keep, tc.tile_pool(name="sums", bufs=2) as sums, tc.tile_pool(
-        name="work", bufs=4
+        name="work", bufs=6
     ) as work, tc.psum_pool(name="turned", bufs=5) as turned_pool, tc.psum_pool(name="product", bufs=1) as product_pool:
         adj = [keep.tile([P, NODES], BF16, name="adj%d" % i) for i in range(ROW_TILES)]
         x_raw = keep.tile([P, PACK, FEATURES], BF16, name="x_raw")
@@ -168,15 +168,15 @@ def tile_gcn_s_kernel(tc, globalAdj, inputs, batch_size, output_dim, client, out
             y = keep.tile([P, batch_size, n, output_dim], F32, name="y%d" % g)
             nc.scalar.copy(out=y[:].rearrange("p b t f -> p t b f"), in_=banks[first // PACK][:, first % PACK : first % PACK + n, :].rearrange("p t (b f) -> p t b f", b=batch_size))
             rows = out[:, client_rows(first), :].rearrange("b (p t) f -> p b t f", t=PACK)
-            nc.scalar.dma_start(out=rows[:, :, first % PACK : first % PACK + n, :], in_=y[:])
+            nc.sync.dma_start(out=rows[:, :, first % PACK : first % PACK + n, :], in_=y[:])
 
         make_identity(nc, ident[:])
         with tc.manual_schedule():
+            nc.sync.dma_start(out=x_raw[:], in_=inputs.rearrange("(p t) f -> p t f", t=PACK))
             load(0)
             load(1)
             load(2)
             load(3)
-            nc.sync.dma_start(out=x_raw[:], in_=inputs.rearrange("(p t) f -> p t f", t=PACK))
             load(4)
             load(5)
             load(6)
@@ -187,25 +187,24 @@ def tile_gcn_s_kernel(tc, globalAdj, inputs, batch_size, output_dim, client, out
             load(11)
             nc.vector.memset(one[:], 1.0)
             nc.scalar.activation(out=warm[:], in_=one[:], func=ACT.Abs_reciprocal_sqrt)
-            add_loop_early(0)
-            add_loop_early(1)
+            nc.vector.tensor_copy(out=x_grouped[:], in_=x_raw[:].rearrange("p t f -> p f t"))
+            nc.vector.quantize_mx(out=x_codes[:].bitcast(FP8X4), scales=x_scales[:], in_=x_grouped[:].rearrange("p f t -> p (f t)"))
             row_sum(0)
             inverse_root(0)
             scale_rows(0, nc.gpsimd)
-            scale_looped(0)
             row_sum(1)
             inverse_root(1)
             scale_rows(1, nc.gpsimd)
-            scale_looped(1)
             row_sum(2)
             inverse_root(2)
             scale_rows(2, nc.gpsimd)
+            self_loop(0)
             turn(0)
             row_sum(3)
             inverse_root(3)
             scale_rows(3, nc.gpsimd)
+            self_loop(1)
             turn(1)
-            nc.gpsimd.tensor_scalar(out=x_grouped[:], in0=x_raw[:].rearrange("p t f -> p f t"), scalar1=1.0, scalar2=0.0, op0=ALU.mult, op1=ALU.add)
             scale_columns(0)
             self_loop(2)
             row_sum(4)
@@ -217,7 +216,6 @@ def tile_gcn_s_kernel(tc, globalAdj, inputs, batch_size, output_dim, client, out
             turn(3)
             turn(4)
             scale_columns(1)
-            nc.vector.quantize_mx(out=x_codes[:].bitcast(FP8X4), scales=x_scales[:], in_=x_grouped[:].rearrange("p f t -> p (f t)"))
             inverse_root(5)
             scale_rows(5, nc.gpsimd)
             row_sum(6)

@@ -33,7 +33,7 @@ def tile_gcn_s_kernel(tc, globalAdj, inputs, batch_size, output_dim, client, out
     share = {0: 1024, 1: 1024, 2: 1024, 3: 1024, 4: 0, 5: 1536, 6: 0, 7: 0, 8: 1536, 9: 0, 10: 768, 11: 1024}
 
     with tc.tile_pool(name="keep", bufs=1) as keep, tc.tile_pool(name="sums", bufs=2) as sums, tc.tile_pool(
-        name="work", bufs=6
+        name="work", bufs=8
     ) as work, tc.psum_pool(name="turned", bufs=5) as turned_pool, tc.psum_pool(name="product", bufs=1) as product_pool:
         adj = [keep.tile([P, NODES], BF16, name="adj%d" % i) for i in range(ROW_TILES)]
         x_raw = keep.tile([P, PACK, FEATURES], BF16, name="x_raw")
@@ -50,7 +50,7 @@ def tile_gcn_s_kernel(tc, globalAdj, inputs, batch_size, output_dim, client, out
         runs = [range(0, 4), range(4, 8), range(8, 10), range(10, 12)]
         banks = [product_pool.tile([P, PACK, FEATURES], F32, name="product%d" % c) for c in range(len(clients))]
 
-        looped = {}
+        looped, both, outer = {}, {}, {}
         scaled, turned, whole, grouped, codes, scales = {}, {}, {}, {}, {}, {}
 
         def load(i):
@@ -73,15 +73,11 @@ def tile_gcn_s_kernel(tc, globalAdj, inputs, batch_size, output_dim, client, out
             unused = sums.tile([P, NODES], BF16, name="unused_s")
             nc.scalar.activation(out=unused[:, columns], in_=adj[i][:, columns], func=ACT.Copy, accum_out=sum_s[:, i, 0:1])
 
-        def row_sum(i):
-            if share[i] > 0:
-                sum_on_vector(i, slice(0, share[i]))
-            if share[i] < NODES:
-                sum_on_scalar(i, slice(share[i], NODES))
-
         def inverse_root(i):
             source, bias = sum_v, 0.0
-            if 0 < share[i] < NODES:
+            if i in outer:
+                bias = sum_s[:, i, 0:1]
+            elif 0 < share[i] < NODES:
                 bias = sum_s[:, i, 0:1]
             elif share[i] == 0:
                 source, bias = sum_s, 1.0
@@ -98,25 +94,19 @@ def tile_gcn_s_kernel(tc, globalAdj, inputs, batch_size, output_dim, client, out
                 op1=ALU.add,
             )
 
+        def scale_rows_s(i):
+            scaled[i] = work.tile([P, PACK, P], F32, name="scaled")
+            nc.scalar.activation(
+                out=scaled[i][:],
+                in_=adj[i][:, mine].rearrange("n (p t) -> n t p", t=PACK),
+                func=ACT.Copy,
+                scale=dinv[:, i : i + 1],
+            )
+
         def self_loop(i):
             block = scaled[i][:, i, :]
             nc.vector.scalar_tensor_tensor(
                 out=block, in0=ident[:], scalar=dinv[:, i : i + 1], in1=block, op0=ALU.mult, op1=ALU.add
-            )
-
-        def add_loop_early(i):
-            looped[i] = keep.tile([P, P], F32, name="looped%d" % i)
-            block = adj[i][:, mine].rearrange("n (p t) -> n t p", t=PACK)[:, i, :]
-            nc.gpsimd.tensor_tensor(out=looped[i][:], in0=block, in1=ident[:], op=ALU.add)
-
-        def scale_looped(i):
-            nc.gpsimd.tensor_scalar(
-                out=scaled[i][:, i, :],
-                in0=looped[i][:],
-                scalar1=dinv[:, i : i + 1],
-                scalar2=0.0,
-                op0=ALU.mult,
-                op1=ALU.add,
             )
 
         def turn(i):
@@ -124,14 +114,19 @@ def tile_gcn_s_kernel(tc, globalAdj, inputs, batch_size, output_dim, client, out
             for t in range(PACK):
                 nc.tensor.transpose(turned[i][:, t, :], scaled[i][:, t, :], ident[:])
 
-        def scale_columns(i):
-            if i % 2 == 0:
+        def new_pair(i):
+            first = i - i % 2
+            if first not in whole:
                 pair = work.tile([P, 2, P, PACK], BF16, align_bytes=64, name="pair")
                 pair_codes = work.tile([P, 2, P], U32, align_bytes=64, name="pair_codes")
                 pair_scales = work.tile([P, 2, P], U8, align_bytes=64, name="pair_scales")
                 for j in range(2):
-                    grouped[i + j], codes[i + j], scales[i + j] = pair[:, j], pair_codes[:, j, :], pair_scales[:, j, :]
-                whole[i] = (pair, pair_codes, pair_scales)
+                    grouped[first + j] = pair[:, j]
+                    codes[first + j], scales[first + j] = pair_codes[:, j, :], pair_scales[:, j, :]
+                whole[first] = (pair, pair_codes, pair_scales)
+
+        def scale_columns(i):
+            new_pair(i)
             nc.vector.tensor_tensor(
                 out=grouped[i],
                 in0=turned[i][:].rearrange("p t n -> p n t"),
@@ -163,10 +158,10 @@ def tile_gcn_s_kernel(tc, globalAdj, inputs, batch_size, output_dim, client, out
                 stop=True,
             )
 
-        def store(g):
+        def store(g, engine_copy):
             n, first = len(runs[g]), runs[g][0]
             y = keep.tile([P, batch_size, n, output_dim], F32, name="y%d" % g)
-            nc.scalar.copy(out=y[:].rearrange("p b t f -> p t b f"), in_=banks[first // PACK][:, first % PACK : first % PACK + n, :].rearrange("p t (b f) -> p t b f", b=batch_size))
+            engine_copy(out=y[:].rearrange("p b t f -> p t b f"), in_=banks[first // PACK][:, first % PACK : first % PACK + n, :].rearrange("p t (b f) -> p t b f", b=batch_size))
             rows = out[:, client_rows(first), :].rearrange("b (p t) f -> p b t f", t=PACK)
             nc.sync.dma_start(out=rows[:, :, first % PACK : first % PACK + n, :], in_=y[:])
 
@@ -187,92 +182,98 @@ def tile_gcn_s_kernel(tc, globalAdj, inputs, batch_size, output_dim, client, out
             load(11)
             nc.vector.memset(one[:], 1.0)
             nc.scalar.activation(out=warm[:], in_=one[:], func=ACT.Abs_reciprocal_sqrt)
+            sum_on_scalar(0, slice(share[0], NODES))
             nc.vector.tensor_copy(out=x_grouped[:], in_=x_raw[:].rearrange("p t f -> p f t"))
             nc.vector.quantize_mx(out=x_codes[:].bitcast(FP8X4), scales=x_scales[:], in_=x_grouped[:].rearrange("p f t -> p (f t)"))
-            row_sum(0)
+            sum_on_vector(0, slice(0, share[0]))
             inverse_root(0)
+            sum_on_scalar(1, slice(share[1], NODES))
             scale_rows(0, nc.gpsimd)
-            row_sum(1)
+            sum_on_vector(1, slice(0, share[1]))
             inverse_root(1)
+            sum_on_scalar(2, slice(share[2], NODES))
             scale_rows(1, nc.gpsimd)
-            row_sum(2)
+            sum_on_vector(2, slice(0, share[2]))
             inverse_root(2)
+            sum_on_scalar(3, slice(share[3], NODES))
             scale_rows(2, nc.gpsimd)
             self_loop(0)
             turn(0)
-            row_sum(3)
+            sum_on_vector(3, slice(0, share[3]))
             inverse_root(3)
+            sum_on_scalar(4, slice(share[4], NODES))
+            inverse_root(4)
             scale_rows(3, nc.gpsimd)
+            scale_rows(4, nc.gpsimd)
             self_loop(1)
             turn(1)
             scale_columns(0)
             self_loop(2)
-            row_sum(4)
-            inverse_root(4)
-            scale_rows(4, nc.gpsimd)
             turn(2)
-            row_sum(5)
+            sum_on_vector(5, slice(0, share[5]))
+            inverse_root(5)
+            sum_on_scalar(6, slice(share[6], NODES))
+            inverse_root(6)
+            sum_on_scalar(7, slice(share[7], NODES))
+            inverse_root(7)
+            scale_rows(5, nc.gpsimd)
+            scale_rows(6, nc.gpsimd)
+            scale_rows(7, nc.gpsimd)
             self_loop(3)
             turn(3)
             turn(4)
-            scale_columns(1)
-            inverse_root(5)
-            scale_rows(5, nc.gpsimd)
-            row_sum(6)
-            inverse_root(6)
-            scale_rows(6, nc.gpsimd)
             turn(5)
+            turn(6)
+            scale_columns(1)
             scale_columns(2)
             quantise_pair(0)
             multiply(0)
             multiply(1)
-            row_sum(7)
-            inverse_root(7)
-            scale_rows(7, nc.gpsimd)
-            turn(6)
             scale_columns(3)
-            row_sum(8)
-            turn(7)
+            sum_on_vector(8, slice(0, share[8]))
+            inverse_root(8)
+            sum_on_scalar(9, slice(share[9], NODES))
+            inverse_root(9)
+            sum_on_scalar(10, slice(share[10], NODES))
+            scale_rows(8, nc.gpsimd)
+            scale_rows(9, nc.gpsimd)
             scale_columns(4)
             quantise_pair(2)
             multiply(2)
             multiply(3)
-            inverse_root(8)
-            scale_rows(8, nc.gpsimd)
-            row_sum(9)
-            inverse_root(9)
-            scale_rows(9, nc.gpsimd)
+            turn(7)
             turn(8)
-            scale_columns(5)
-            row_sum(10)
-            inverse_root(10)
-            scale_rows(10, nc.gpsimd)
             turn(9)
+            scale_columns(5)
+            sum_on_vector(10, slice(0, share[10]))
+            inverse_root(10)
+            sum_on_scalar(11, slice(share[11], NODES))
+            scale_rows(10, nc.gpsimd)
             scale_columns(6)
+            turn(10)
             quantise_pair(4)
+            sum_on_vector(11, slice(0, share[11]))
+            inverse_root(11)
+            scale_rows_s(11)
+            store(0, nc.scalar.copy)
+            turn(11)
             multiply(4)
             multiply(5)
-            row_sum(11)
-            inverse_root(11)
-            scale_rows(11, nc.gpsimd)
-            turn(10)
             scale_columns(7)
-            turn(11)
             scale_columns(8)
             quantise_pair(6)
             multiply(6)
             multiply(7)
             scale_columns(9)
+            store(1, nc.scalar.copy)
             scale_columns(10)
             quantise_pair(8)
             multiply(8)
             multiply(9)
             scale_columns(11)
+            store(2, nc.scalar.copy)
             quantise(10)
             multiply(10)
             quantise(11)
             multiply(11)
-            store(0)
-            store(1)
-            store(2)
-            store(3)
+            store(3, nc.scalar.copy)

@@ -103,10 +103,12 @@ def tile_gcn_s_kernel(tc, globalAdj, inputs, batch_size, output_dim, client, out
                 scale=dinv[:, i : i + 1],
             )
 
+        ident_psum = banks[-1][:, 0, :]
+
         def self_loop(i):
             block = scaled[i][:, i, :]
             nc.vector.scalar_tensor_tensor(
-                out=block, in0=ident[:], scalar=dinv[:, i : i + 1], in1=block, op0=ALU.mult, op1=ALU.add
+                out=block, in0=ident_psum, scalar=dinv[:, i : i + 1], in1=block, op0=ALU.mult, op1=ALU.add
             )
 
         def turn(i):
@@ -114,19 +116,19 @@ def tile_gcn_s_kernel(tc, globalAdj, inputs, batch_size, output_dim, client, out
             for t in range(PACK):
                 nc.tensor.transpose(turned[i][:, t, :], scaled[i][:, t, :], ident[:])
 
-        def new_pair(i):
-            first = i - i % 2
+        def new_group(i):
+            first = i - i % PACK
             if first not in whole:
-                pair = work.tile([P, 2, P, PACK], BF16, align_bytes=64, name="pair")
-                pair_codes = work.tile([P, 2, P], U32, align_bytes=64, name="pair_codes")
-                pair_scales = work.tile([P, 2, P], U8, align_bytes=64, name="pair_scales")
-                for j in range(2):
-                    grouped[first + j] = pair[:, j]
-                    codes[first + j], scales[first + j] = pair_codes[:, j, :], pair_scales[:, j, :]
-                whole[first] = (pair, pair_codes, pair_scales)
+                group = work.tile([P, PACK, P, PACK], BF16, align_bytes=64, name="group")
+                group_codes = work.tile([P, PACK, P], U32, align_bytes=64, name="group_codes")
+                group_scales = work.tile([P, PACK, P], U8, align_bytes=64, name="group_scales")
+                for j in range(PACK):
+                    grouped[first + j] = group[:, j]
+                    codes[first + j], scales[first + j] = group_codes[:, j, :], group_scales[:, j, :]
+                whole[first] = (group, group_codes, group_scales)
 
         def scale_columns(i):
-            new_pair(i)
+            new_group(i)
             nc.vector.tensor_tensor(
                 out=grouped[i],
                 in0=turned[i][:].rearrange("p t n -> p n t"),
@@ -134,17 +136,13 @@ def tile_gcn_s_kernel(tc, globalAdj, inputs, batch_size, output_dim, client, out
                 op=ALU.mult,
             )
 
-        def quantise_pair(i):
-            pair, pair_codes, pair_scales = whole[i]
+        def quantise(i, n):
+            group, group_codes, group_scales = whole[i - i % PACK]
+            j = slice(i % PACK, i % PACK + n)
             nc.vector.quantize_mx(
-                out=pair_codes[:].rearrange("p j n -> p (j n)").bitcast(FP8X4),
-                scales=pair_scales[:].rearrange("p j n -> p (j n)"),
-                in_=pair[:].rearrange("p j n t -> p (j n t)"),
-            )
-
-        def quantise(i):
-            nc.vector.quantize_mx(
-                out=codes[i].bitcast(FP8X4), scales=scales[i], in_=grouped[i].rearrange("p n t -> p (n t)")
+                out=group_codes[:, j].rearrange("p j n -> p (j n)").bitcast(FP8X4),
+                scales=group_scales[:, j].rearrange("p j n -> p (j n)"),
+                in_=group[:, j].rearrange("p j n t -> p (j n t)"),
             )
 
         def multiply(i):
@@ -183,6 +181,7 @@ def tile_gcn_s_kernel(tc, globalAdj, inputs, batch_size, output_dim, client, out
             nc.vector.memset(one[:], 1.0)
             nc.scalar.activation(out=warm[:], in_=one[:], func=ACT.Abs_reciprocal_sqrt)
             sum_on_scalar(0, slice(share[0], NODES))
+            nc.tensor.transpose(ident_psum, ident[:], ident[:])
             nc.vector.tensor_copy(out=x_grouped[:], in_=x_raw[:].rearrange("p t f -> p f t"))
             nc.vector.quantize_mx(out=x_codes[:].bitcast(FP8X4), scales=x_scales[:], in_=x_grouped[:].rearrange("p f t -> p (f t)"))
             sum_on_vector(0, slice(0, share[0]))
@@ -226,9 +225,6 @@ def tile_gcn_s_kernel(tc, globalAdj, inputs, batch_size, output_dim, client, out
             turn(6)
             scale_columns(1)
             scale_columns(2)
-            quantise_pair(0)
-            multiply(0)
-            multiply(1)
             scale_columns(3)
             sum_on_vector(8, slice(0, share[8]))
             inverse_root(8)
@@ -238,7 +234,9 @@ def tile_gcn_s_kernel(tc, globalAdj, inputs, batch_size, output_dim, client, out
             scale_rows(8, nc.gpsimd)
             scale_rows(9, nc.gpsimd)
             scale_columns(4)
-            quantise_pair(2)
+            quantise(0, 4)
+            multiply(0)
+            multiply(1)
             multiply(2)
             multiply(3)
             turn(7)
@@ -251,29 +249,28 @@ def tile_gcn_s_kernel(tc, globalAdj, inputs, batch_size, output_dim, client, out
             scale_rows(10, nc.gpsimd)
             scale_columns(6)
             turn(10)
-            quantise_pair(4)
             sum_on_vector(11, slice(0, share[11]))
             inverse_root(11)
             scale_rows_s(11)
             store(0, nc.scalar.copy)
             turn(11)
-            multiply(4)
-            multiply(5)
             scale_columns(7)
             scale_columns(8)
-            quantise_pair(6)
+            quantise(4, 4)
+            multiply(4)
+            multiply(5)
             multiply(6)
             multiply(7)
             scale_columns(9)
             store(1, nc.scalar.copy)
             scale_columns(10)
-            quantise_pair(8)
+            quantise(8, 2)
             multiply(8)
             multiply(9)
             scale_columns(11)
             store(2, nc.scalar.copy)
-            quantise(10)
+            quantise(10, 1)
             multiply(10)
-            quantise(11)
+            quantise(11, 1)
             multiply(11)
             store(3, nc.scalar.copy)

@@ -30,7 +30,7 @@ def tile_gcn_s_kernel(tc, globalAdj, inputs, batch_size, output_dim, client, out
         c = clients[i // PACK]
         return slice(c * CLIENT, (c + 1) * CLIENT)
 
-    share = {0: 1024, 1: 1024, 2: 1024, 3: 1024, 4: 0, 5: 1536, 6: 0, 7: 0, 8: 1536, 9: 0, 10: 768, 11: 1024}
+    share = {0: 1024, 1: 1024, 2: 1024, 3: 1024, 4: 512, 5: 0, 6: 1536, 7: 0, 8: 1536, 9: 0, 10: 512, 11: 512}
 
     with tc.tile_pool(name="keep", bufs=1) as keep, tc.tile_pool(name="sums", bufs=2) as sums, tc.tile_pool(
         name="work", bufs=8
@@ -43,15 +43,18 @@ def tile_gcn_s_kernel(tc, globalAdj, inputs, batch_size, output_dim, client, out
         x_grouped = keep.tile([P, FEATURES, PACK], BF16, align_bytes=64, name="x_grouped")
         x_codes = keep.tile([P, FEATURES], U32, align_bytes=64, name="x_codes")
         x_scales = keep.tile([P, FEATURES], U8, align_bytes=64, name="x_scales")
+        grouped = keep.tile([P, ROW_TILES, P, PACK], BF16, align_bytes=64, name="grouped")
+        codes = keep.tile([P, ROW_TILES, P], U32, align_bytes=64, name="codes")
+        scales = keep.tile([P, ROW_TILES, P], U8, align_bytes=64, name="scales")
         sum_v = keep.tile([P, ROW_TILES, 8], F32, name="sum_v")
         sum_s = keep.tile([P, ROW_TILES, 8], F32, name="sum_s")
         dinv = keep.tile([P, ROW_TILES], F32, name="dinv")
 
         runs = [range(0, 4), range(4, 8), range(8, 10), range(10, 12)]
-        banks = [product_pool.tile([P, PACK, FEATURES], F32, name="product%d" % c) for c in range(len(clients))]
+        banks = [product_pool.tile([P, PACK, FEATURES], F32, name="product%d" % b) for b in range(3)]
+        place = {i: banks[g % len(banks)][:, i - run.start, :] for g, run in enumerate(runs) for i in run}
 
-        looped, both, outer = {}, {}, {}
-        scaled, turned, whole, grouped, codes, scales = {}, {}, {}, {}, {}, {}
+        scaled, turned = {}, {}
 
         def load(i):
             rows = globalAdj[client_rows(i), :].rearrange("(p t) j -> p t j", t=PACK)
@@ -75,9 +78,7 @@ def tile_gcn_s_kernel(tc, globalAdj, inputs, batch_size, output_dim, client, out
 
         def inverse_root(i):
             source, bias = sum_v, 0.0
-            if i in outer:
-                bias = sum_s[:, i, 0:1]
-            elif 0 < share[i] < NODES:
+            if 0 < share[i] < NODES:
                 bias = sum_s[:, i, 0:1]
             elif share[i] == 0:
                 source, bias = sum_s, 1.0
@@ -116,40 +117,27 @@ def tile_gcn_s_kernel(tc, globalAdj, inputs, batch_size, output_dim, client, out
             for t in range(PACK):
                 nc.tensor.transpose(turned[i][:, t, :], scaled[i][:, t, :], ident[:])
 
-        def new_group(i):
-            first = i - i % PACK
-            if first not in whole:
-                group = work.tile([P, PACK, P, PACK], BF16, align_bytes=64, name="group")
-                group_codes = work.tile([P, PACK, P], U32, align_bytes=64, name="group_codes")
-                group_scales = work.tile([P, PACK, P], U8, align_bytes=64, name="group_scales")
-                for j in range(PACK):
-                    grouped[first + j] = group[:, j]
-                    codes[first + j], scales[first + j] = group_codes[:, j, :], group_scales[:, j, :]
-                whole[first] = (group, group_codes, group_scales)
-
         def scale_columns(i):
-            new_group(i)
             nc.vector.tensor_tensor(
-                out=grouped[i],
+                out=grouped[:, i],
                 in0=turned[i][:].rearrange("p t n -> p n t"),
                 in1=dinv[:, 0:PACK].unsqueeze(1).to_broadcast([P, P, PACK]),
                 op=ALU.mult,
             )
 
         def quantise(i, n):
-            group, group_codes, group_scales = whole[i - i % PACK]
-            j = slice(i % PACK, i % PACK + n)
+            tiles = slice(i, i + n)
             nc.vector.quantize_mx(
-                out=group_codes[:, j].rearrange("p j n -> p (j n)").bitcast(FP8X4),
-                scales=group_scales[:, j].rearrange("p j n -> p (j n)"),
-                in_=group[:, j].rearrange("p j n t -> p (j n t)"),
+                out=codes[:, tiles].rearrange("p i n -> p (i n)").bitcast(FP8X4),
+                scales=scales[:, tiles].rearrange("p i n -> p (i n)"),
+                in_=grouped[:, tiles].rearrange("p i n t -> p (i n t)"),
             )
 
         def multiply(i):
             nc.tensor.matmul_mx(
-                out=banks[i // PACK][:, i % PACK, :],
-                lhsT=codes[i].bitcast(FP8X4),
-                lhsT_scale=scales[i],
+                out=place[i],
+                lhsT=codes[:, i].bitcast(FP8X4),
+                lhsT_scale=scales[:, i],
                 rhs=x_codes[:].bitcast(FP8X4),
                 rhs_scale=x_scales[:],
                 start=True,
@@ -159,7 +147,7 @@ def tile_gcn_s_kernel(tc, globalAdj, inputs, batch_size, output_dim, client, out
         def store(g, engine_copy):
             n, first = len(runs[g]), runs[g][0]
             y = keep.tile([P, batch_size, n, output_dim], F32, name="y%d" % g)
-            engine_copy(out=y[:].rearrange("p b t f -> p t b f"), in_=banks[first // PACK][:, first % PACK : first % PACK + n, :].rearrange("p t (b f) -> p t b f", b=batch_size))
+            engine_copy(out=y[:].rearrange("p b t f -> p t b f"), in_=banks[g % len(banks)][:, 0:n, :].rearrange("p t (b f) -> p t b f", b=batch_size))
             rows = out[:, client_rows(first), :].rearrange("b (p t) f -> p b t f", t=PACK)
             nc.sync.dma_start(out=rows[:, :, first % PACK : first % PACK + n, :], in_=y[:])
 
@@ -201,17 +189,19 @@ def tile_gcn_s_kernel(tc, globalAdj, inputs, batch_size, output_dim, client, out
             sum_on_vector(3, slice(0, share[3]))
             inverse_root(3)
             sum_on_scalar(4, slice(share[4], NODES))
-            inverse_root(4)
             scale_rows(3, nc.gpsimd)
-            scale_rows(4, nc.gpsimd)
             self_loop(1)
             turn(1)
+            sum_on_vector(4, slice(0, share[4]))
+            inverse_root(4)
+            scale_rows(4, nc.gpsimd)
             scale_columns(0)
             self_loop(2)
             turn(2)
-            sum_on_vector(5, slice(0, share[5]))
+            scale_columns(1)
+            sum_on_vector(6, slice(0, share[6]))
+            sum_on_scalar(5, slice(share[5], NODES))
             inverse_root(5)
-            sum_on_scalar(6, slice(share[6], NODES))
             inverse_root(6)
             sum_on_scalar(7, slice(share[7], NODES))
             inverse_root(7)
@@ -223,7 +213,6 @@ def tile_gcn_s_kernel(tc, globalAdj, inputs, batch_size, output_dim, client, out
             turn(4)
             turn(5)
             turn(6)
-            scale_columns(1)
             scale_columns(2)
             scale_columns(3)
             sum_on_vector(8, slice(0, share[8]))
@@ -234,11 +223,6 @@ def tile_gcn_s_kernel(tc, globalAdj, inputs, batch_size, output_dim, client, out
             scale_rows(8, nc.gpsimd)
             scale_rows(9, nc.gpsimd)
             scale_columns(4)
-            quantise(0, 4)
-            multiply(0)
-            multiply(1)
-            multiply(2)
-            multiply(3)
             turn(7)
             turn(8)
             turn(9)
@@ -248,19 +232,24 @@ def tile_gcn_s_kernel(tc, globalAdj, inputs, batch_size, output_dim, client, out
             sum_on_scalar(11, slice(share[11], NODES))
             scale_rows(10, nc.gpsimd)
             scale_columns(6)
-            turn(10)
             sum_on_vector(11, slice(0, share[11]))
             inverse_root(11)
             scale_rows_s(11)
-            store(0, nc.scalar.copy)
-            turn(11)
             scale_columns(7)
+            quantise(0, 4)
+            multiply(0)
+            multiply(1)
+            multiply(2)
+            multiply(3)
+            store(0, nc.scalar.copy)
+            turn(10)
             scale_columns(8)
             quantise(4, 4)
             multiply(4)
             multiply(5)
             multiply(6)
             multiply(7)
+            turn(11)
             scale_columns(9)
             store(1, nc.scalar.copy)
             scale_columns(10)
@@ -273,4 +262,4 @@ def tile_gcn_s_kernel(tc, globalAdj, inputs, batch_size, output_dim, client, out
             multiply(10)
             quantise(11, 1)
             multiply(11)
-            store(3, nc.scalar.copy)
+            store(3, nc.vector.tensor_copy)

@@ -30,7 +30,7 @@ def tile_gcn_s_kernel(tc, globalAdj, inputs, batch_size, output_dim, client, out
         c = clients[i // PACK]
         return slice(c * CLIENT, (c + 1) * CLIENT)
 
-    share = {0: 1024, 1: 1024, 2: 1024, 3: 1024, 4: 512, 5: 0, 6: 1536, 7: 0, 8: 1536, 9: 0, 10: 512, 11: 512}
+    share = {0: 1024, 1: 1024, 2: 1024, 3: 1024, 4: 1024, 5: 0, 6: 1536, 7: 0, 8: 1536, 9: 0, 10: 1024, 11: 512}
 
     with tc.tile_pool(name="keep", bufs=1) as keep, tc.tile_pool(name="sums", bufs=2) as sums, tc.tile_pool(
         name="work", bufs=8

import concourse.mybir as mybir
from concourse.masks import make_identity

BF16 = mybir.dt.bfloat16
F32 = mybir.dt.float32
U32 = mybir.dt.uint32
U8 = mybir.dt.uint8
FP8X4 = mybir.dt.float8_e4m3fn_x4
ALU = mybir.AluOpType
ACT = mybir.ActivationFunctionType

P = 128
PACK = 4
NODES = 1536
CLIENT = P * PACK
FEATURES = 128
ROW_TILES = NODES // P

FLOPS = 2 * NODES * CLIENT * FEATURES


def tile_gcn_s_kernel(tc, globalAdj, inputs, batch_size, output_dim, client, out):
    nc = tc.nc
    assert batch_size * output_dim == FEATURES

    clients = [client] + [c for c in range(NODES // CLIENT) if c != client]
    mine = slice(client * CLIENT, (client + 1) * CLIENT)

    def client_rows(i):
        c = clients[i // PACK]
        return slice(c * CLIENT, (c + 1) * CLIENT)

    share = {0: 1024, 1: 1024, 2: 1024, 3: 1024, 4: 1024, 5: 0, 6: 1536, 7: 0, 8: 1536, 9: 0, 10: 1024, 11: 512}

    with tc.tile_pool(name="keep", bufs=1) as keep, tc.tile_pool(name="sums", bufs=2) as sums, tc.tile_pool(
        name="work", bufs=8
    ) as work, tc.psum_pool(name="turned", bufs=5) as turned_pool, tc.psum_pool(name="product", bufs=1) as product_pool:
        adj = [keep.tile([P, NODES], BF16, name="adj%d" % i) for i in range(ROW_TILES)]
        x_raw = keep.tile([P, PACK, FEATURES], BF16, name="x_raw")
        ident = keep.tile([P, P], F32, name="ident")
        one = keep.tile([P, 1], F32, name="one")
        warm = keep.tile([P, 1], F32, name="warm")
        x_grouped = keep.tile([P, FEATURES, PACK], BF16, align_bytes=64, name="x_grouped")
        x_codes = keep.tile([P, FEATURES], U32, align_bytes=64, name="x_codes")
        x_scales = keep.tile([P, FEATURES], U8, align_bytes=64, name="x_scales")
        grouped = keep.tile([P, ROW_TILES, P, PACK], BF16, align_bytes=64, name="grouped")
        codes = keep.tile([P, ROW_TILES, P], U32, align_bytes=64, name="codes")
        scales = keep.tile([P, ROW_TILES, P], U8, align_bytes=64, name="scales")
        sum_v = keep.tile([P, ROW_TILES, 8], F32, name="sum_v")
        sum_s = keep.tile([P, ROW_TILES, 8], F32, name="sum_s")
        dinv = keep.tile([P, ROW_TILES], F32, name="dinv")

        runs = [range(0, 4), range(4, 8), range(8, 10), range(10, 12)]
        banks = [product_pool.tile([P, PACK, FEATURES], F32, name="product%d" % b) for b in range(3)]
        place = {i: banks[g % len(banks)][:, i - run.start, :] for g, run in enumerate(runs) for i in run}

        scaled, turned = {}, {}

        def load(i):
            rows = globalAdj[client_rows(i), :].rearrange("(p t) j -> p t j", t=PACK)
            nc.sync.dma_start(out=adj[i][:], in_=rows[:, i % PACK, :])

        def sum_on_vector(i, columns):
            unused = sums.tile([P, NODES], BF16, name="unused_v")
            nc.vector.tensor_scalar(
                out=unused[:, columns],
                in0=adj[i][:, columns],
                scalar1=1.0,
                scalar2=1.0,
                op0=ALU.mult,
                op1=ALU.add,
                accum_out=sum_v[:, i, 0:1],
            )

        def sum_on_scalar(i, columns):
            unused = sums.tile([P, NODES], BF16, name="unused_s")
            nc.scalar.activation(out=unused[:, columns], in_=adj[i][:, columns], func=ACT.Copy, accum_out=sum_s[:, i, 0:1])

        def inverse_root(i):
            source, bias = sum_v, 0.0
            if 0 < share[i] < NODES:
                bias = sum_s[:, i, 0:1]
            elif share[i] == 0:
                source, bias = sum_s, 1.0
            nc.scalar.activation(out=dinv[:, i : i + 1], in_=source[:, i, 0:1], func=ACT.Abs_reciprocal_sqrt, bias=bias)

        def scale_rows(i, engine):
            scaled[i] = work.tile([P, PACK, P], F32, name="scaled")
            engine.tensor_scalar(
                out=scaled[i][:],
                in0=adj[i][:, mine].rearrange("n (p t) -> n t p", t=PACK),
                scalar1=dinv[:, i : i + 1],
                scalar2=0.0,
                op0=ALU.mult,
                op1=ALU.add,
            )

        def scale_rows_s(i):
            scaled[i] = work.tile([P, PACK, P], F32, name="scaled")
            nc.scalar.activation(
                out=scaled[i][:],
                in_=adj[i][:, mine].rearrange("n (p t) -> n t p", t=PACK),
                func=ACT.Copy,
                scale=dinv[:, i : i + 1],
            )

        ident_psum = banks[-1][:, 0, :]

        def self_loop(i):
            block = scaled[i][:, i, :]
            nc.vector.scalar_tensor_tensor(
                out=block, in0=ident_psum, scalar=dinv[:, i : i + 1], in1=block, op0=ALU.mult, op1=ALU.add
            )

        def turn(i):
            turned[i] = turned_pool.tile([P, PACK, P], F32, name="turned")
            for t in range(PACK):
                nc.tensor.transpose(turned[i][:, t, :], scaled[i][:, t, :], ident[:])

        def scale_columns(i):
            nc.vector.tensor_tensor(
                out=grouped[:, i],
                in0=turned[i][:].rearrange("p t n -> p n t"),
                in1=dinv[:, 0:PACK].unsqueeze(1).to_broadcast([P, P, PACK]),
                op=ALU.mult,
            )

        def quantise(i, n):
            tiles = slice(i, i + n)
            nc.vector.quantize_mx(
                out=codes[:, tiles].rearrange("p i n -> p (i n)").bitcast(FP8X4),
                scales=scales[:, tiles].rearrange("p i n -> p (i n)"),
                in_=grouped[:, tiles].rearrange("p i n t -> p (i n t)"),
            )

        def multiply(i):
            nc.tensor.matmul_mx(
                out=place[i],
                lhsT=codes[:, i].bitcast(FP8X4),
                lhsT_scale=scales[:, i],
                rhs=x_codes[:].bitcast(FP8X4),
                rhs_scale=x_scales[:],
                start=True,
                stop=True,
            )

        def store(g, engine_copy):
            n, first = len(runs[g]), runs[g][0]
            y = keep.tile([P, batch_size, n, output_dim], F32, name="y%d" % g)
            engine_copy(out=y[:].rearrange("p b t f -> p t b f"), in_=banks[g % len(banks)][:, 0:n, :].rearrange("p t (b f) -> p t b f", b=batch_size))
            rows = out[:, client_rows(first), :].rearrange("b (p t) f -> p b t f", t=PACK)
            nc.sync.dma_start(out=rows[:, :, first % PACK : first % PACK + n, :], in_=y[:])

        make_identity(nc, ident[:])
        with tc.manual_schedule():
            nc.sync.dma_start(out=x_raw[:], in_=inputs.rearrange("(p t) f -> p t f", t=PACK))
            load(0)
            load(1)
            load(2)
            load(3)
            load(4)
            load(5)
            load(6)
            load(7)
            load(8)
            load(9)
            load(10)
            load(11)
            nc.vector.memset(one[:], 1.0)
            nc.scalar.activation(out=warm[:], in_=one[:], func=ACT.Abs_reciprocal_sqrt)
            sum_on_scalar(0, slice(share[0], NODES))
            nc.tensor.transpose(ident_psum, ident[:], ident[:])
            nc.vector.tensor_copy(out=x_grouped[:], in_=x_raw[:].rearrange("p t f -> p f t"))
            nc.vector.quantize_mx(out=x_codes[:].bitcast(FP8X4), scales=x_scales[:], in_=x_grouped[:].rearrange("p f t -> p (f t)"))
            sum_on_vector(0, slice(0, share[0]))
            inverse_root(0)
            sum_on_scalar(1, slice(share[1], NODES))
            scale_rows(0, nc.gpsimd)
            sum_on_vector(1, slice(0, share[1]))
            inverse_root(1)
            sum_on_scalar(2, slice(share[2], NODES))
            scale_rows(1, nc.gpsimd)
            sum_on_vector(2, slice(0, share[2]))
            inverse_root(2)
            sum_on_scalar(3, slice(share[3], NODES))
            scale_rows(2, nc.gpsimd)
            self_loop(0)
            turn(0)
            sum_on_vector(3, slice(0, share[3]))
            inverse_root(3)
            sum_on_scalar(4, slice(share[4], NODES))
            scale_rows(3, nc.gpsimd)
            self_loop(1)
            turn(1)
            sum_on_vector(4, slice(0, share[4]))
            inverse_root(4)
            scale_rows(4, nc.gpsimd)
            scale_columns(0)
            self_loop(2)
            turn(2)
            scale_columns(1)
            sum_on_vector(6, slice(0, share[6]))
            sum_on_scalar(5, slice(share[5], NODES))
            inverse_root(5)
            inverse_root(6)
            sum_on_scalar(7, slice(share[7], NODES))
            inverse_root(7)
            scale_rows(5, nc.gpsimd)
            scale_rows(6, nc.gpsimd)
            scale_rows(7, nc.gpsimd)
            self_loop(3)
            turn(3)
            turn(4)
            turn(5)
            turn(6)
            scale_columns(2)
            scale_columns(3)
            sum_on_vector(8, slice(0, share[8]))
            inverse_root(8)
            sum_on_scalar(9, slice(share[9], NODES))
            inverse_root(9)
            sum_on_scalar(10, slice(share[10], NODES))
            scale_rows(8, nc.gpsimd)
            scale_rows(9, nc.gpsimd)
            scale_columns(4)
            turn(7)
            turn(8)
            turn(9)
            scale_columns(5)
            sum_on_vector(10, slice(0, share[10]))
            inverse_root(10)
            sum_on_scalar(11, slice(share[11], NODES))
            scale_rows(10, nc.gpsimd)
            scale_columns(6)
            sum_on_vector(11, slice(0, share[11]))
            inverse_root(11)
            scale_rows_s(11)
            scale_columns(7)
            quantise(0, 4)
            multiply(0)
            multiply(1)
            multiply(2)
            multiply(3)
            store(0, nc.scalar.copy)
            turn(10)
            scale_columns(8)
            quantise(4, 4)
            multiply(4)
            multiply(5)
            multiply(6)
            multiply(7)
            turn(11)
            scale_columns(9)
            store(1, nc.scalar.copy)
            scale_columns(10)
            quantise(8, 2)
            multiply(8)
            multiply(9)
            scale_columns(11)
            store(2, nc.scalar.copy)
            quantise(10, 1)
            multiply(10)
            quantise(11, 1)
            multiply(11)
            store(3, nc.vector.tensor_copy)
